import numpy as np
import ml_dtypes


def mxq(x, axis, fmt="e4m3"):
    dtype, down = {"e4m3": (ml_dtypes.float8_e4m3fn, 7), "e5m2": (ml_dtypes.float8_e5m2, 14)}[fmt]
    v = np.moveaxis(np.asarray(x, np.float32).astype(ml_dtypes.bfloat16).astype(np.float64), axis, -1)
    blocks = v.reshape(v.shape[:-1] + (-1, 32))
    amax = np.abs(blocks).max(-1, keepdims=True)
    byte = np.maximum(np.where(amax > 0, np.frexp(amax)[1] - 1 + 127, 0) - down, 1)
    scale = np.exp2(byte - 127.0)
    codes = (blocks / scale).astype(np.float32).astype(dtype).astype(np.float64)
    return np.moveaxis((codes * scale).reshape(v.shape), -1, axis)


WIDE = False


def mx_kscale(k):
    if not WIDE:
        return np.ones(k)
    levels = np.array([10, -10, 5, -5, 0])
    a = np.random.permutation(np.resize(levels, k // 512 * 4)).reshape(k // 512, 4)
    idx = np.arange(k)
    return np.exp2(a[idx // 512, idx % 128 // 32])


BF16 = ml_dtypes.bfloat16


def bf(x):
    return np.asarray(x, np.float32).astype(BF16)


def f64(x):
    return np.asarray(x).astype(np.float64)


S, E = 1536, 1024


def setup_inputs():
    s, t = mx_kscale(E), mx_kscale(S)
    return {"qm": bf(np.random.standard_normal((S, E)) * 0.4 * s),
            "km": bf(np.random.standard_normal((S, E)) * 0.4 / s * t[:, None]),
            "vm": bf(np.random.standard_normal((S, E)) * 0.4 / t[:, None])}


def reference(qm, km, vm):
    qkm = (mxq(f64(qm), 1, "e4m3") @ mxq(f64(km), 1, "e4m3").T) / np.sqrt(S)
    z = mxq(qkm, 1, "e4m3") @ mxq(f64(vm), 0, "e4m3")
    e = np.exp(z - z.max(-1, keepdims=True))
    return e / e.sum(-1, keepdims=True)

@@ -1,0 +1,246 @@
+import math
+from contextlib import ExitStack
+
+import concourse.mybir as mybir
+from concourse.masks import make_identity
+
+F32 = mybir.dt.float32
+BF16 = mybir.dt.bfloat16
+U32 = mybir.dt.uint32
+U8 = mybir.dt.uint8
+FP8X4 = mybir.dt.float8_e4m3fn_x4
+ACT = mybir.ActivationFunctionType
+ALU = mybir.AluOpType
+AXIS = mybir.AxisListType
+
+S = 1536
+E = 1024
+P = 128
+PACK = 4
+K_PASS = P * PACK
+BANK = 512
+
+GROUPS = S // K_PASS
+TILES = K_PASS // P
+E_PASSES = E // K_PASS
+HALVES = E // BANK
+TILE_WORDS = E // PACK
+
+FLOPS = 2 * S * S * E + 2 * S * S * E
+
+
+def tile_headattetion_pa_kernel(tc, qm, km, vm, out):
+    nc = tc.nc
+    inv_sqrt_s = 1.0 / math.sqrt(S)
+
+    with ExitStack() as ctx:
+        const = ctx.enter_context(tc.tile_pool(name="const", bufs=1))
+        keep = ctx.enter_context(tc.tile_pool(name="keep", bufs=1))
+        raw_pool = ctx.enter_context(tc.tile_pool(name="raw", bufs=3 * GROUPS))
+        stage = ctx.enter_context(tc.tile_pool(name="stage", bufs=3))
+        rows = ctx.enter_context(tc.tile_pool(name="rows", bufs=4))
+        small = ctx.enter_context(tc.tile_pool(name="small", bufs=4))
+        psum = ctx.enter_context(tc.psum_pool(name="psum", bufs=8))
+
+        k_codes = keep.tile([P, GROUPS * TILES * TILE_WORDS], U32, align_bytes=64)
+        k_scales = keep.tile([P, GROUPS * TILES * TILE_WORDS], U8, align_bytes=64)
+        q_codes = keep.tile([P, GROUPS * TILES * TILE_WORDS], U32, align_bytes=64)
+        q_scales = keep.tile([P, GROUPS * TILES * TILE_WORDS], U8, align_bytes=64)
+        v_codes = keep.tile([P, GROUPS * E], U32, align_bytes=64)
+        v_scales = keep.tile([P, GROUPS * E], U8, align_bytes=64)
+        s_codes = keep.tile([P, GROUPS * S], U32, align_bytes=64)
+        s_scales = keep.tile([P, GROUPS * S], U8, align_bytes=64)
+
+        blocks = [(c, g) for g in range(GROUPS) for c in range(GROUPS)]
+        needs = []
+        for c, g in blocks:
+            for operand in (("k", c), ("q", g)):
+                if operand not in needs:
+                    needs.append(operand)
+
+        def load_group(src, group, name):
+            raw = raw_pool.tile([P, TILES * E], BF16, name=name, tag="raw")
+            nc.sync.dma_start(
+                out=raw[:],
+                in_=src[group * K_PASS : (group + 1) * K_PASS, :].rearrange(
+                    "(p t) e -> p (t e)", t=TILES
+                ),
+            )
+            return raw
+
+        raw_tiles = {}
+        for kind, group in needs:
+            src = km if kind == "k" else qm
+            raw_tiles[(kind, group)] = load_group(src, group, "raw_%s%d" % (kind, group))
+        for group in range(GROUPS):
+            raw_tiles[("v", group)] = load_group(vm, group, "raw_v%d" % group)
+
+        ident = const.tile([P, P], F32)
+        make_identity(nc, ident[:])
+
+        warm = const.tile([P, 1], F32)
+        nc.vector.memset(warm[:], 0.0)
+        nc.scalar.activation(out=warm[:], in_=warm[:], func=ACT.Exp)
+
+        def prepare(kind, group):
+            raw_words = raw_tiles[(kind, group)][:].bitcast(F32)
+            codes, scales = (k_codes, k_scales) if kind == "k" else (q_codes, q_scales)
+            grouped = stage.tile([P, TILES * E], BF16, tag="grouped", align_bytes=64)
+            grouped_words = grouped[:].bitcast(F32)
+            words = E // 2
+            for t in range(TILES):
+                bank = psum.tile([P, BANK], F32, name="bank_t", tag="bank")
+                for j in range(words // P):
+                    nc.tensor.transpose(
+                        bank[:, j * P : (j + 1) * P],
+                        raw_words[:, t * words + j * P : t * words + (j + 1) * P],
+                        ident[:],
+                    )
+                dst = grouped_words[:, t * words : (t + 1) * words].rearrange(
+                    "p (a r u) -> p a r u", a=E_PASSES, u=2
+                )
+                src = bank[:].rearrange("p (a u r) -> p a r u", a=E_PASSES, u=2)
+                if t % 2 == 0:
+                    nc.scalar.copy(out=dst, in_=src)
+                else:
+                    nc.vector.tensor_copy(out=dst, in_=src)
+            for t in range(TILES):
+                first = (group * TILES + t) * TILE_WORDS
+                nc.vector.quantize_mx(
+                    out=codes[:, first : first + TILE_WORDS].bitcast(FP8X4),
+                    scales=scales[:, first : first + TILE_WORDS],
+                    in_=grouped[:, t * E : (t + 1) * E],
+                )
+
+        def score_block(c, g):
+            s_grouped = stage.tile([P, TILES * P * PACK], BF16, tag="s_grouped", align_bytes=64)
+            for i in range(TILES):
+                bank = psum.tile([P, BANK], F32, name="bank_s", tag="bank")
+                for t in range(TILES):
+                    for a in range(E_PASSES):
+                        k_first = (c * TILES + t) * TILE_WORDS + a * P
+                        q_first = (g * TILES + i) * TILE_WORDS + a * P
+                        nc.tensor.matmul_mx(
+                            out=bank[:, t * P : (t + 1) * P],
+                            lhsT=k_codes[:, k_first : k_first + P].bitcast(FP8X4),
+                            lhsT_scale=k_scales[:, k_first : k_first + P],
+                            rhs=q_codes[:, q_first : q_first + P].bitcast(FP8X4),
+                            rhs_scale=q_scales[:, q_first : q_first + P],
+                            start=(a == 0),
+                            stop=(a == E_PASSES - 1),
+                        )
+                nc.scalar.activation(
+                    out=s_grouped[:, i * BANK : (i + 1) * BANK].rearrange(
+                        "p (n t) -> p n t", t=TILES
+                    ),
+                    in_=bank[:].rearrange("p (t n) -> p n t", t=TILES),
+                    func=ACT.Copy,
+                    scale=inv_sqrt_s,
+                )
+            return s_grouped
+
+        def quantise_block(c, g, s_grouped):
+            first = (c * GROUPS + g) * K_PASS
+            nc.vector.quantize_mx(
+                out=s_codes[:, first : first + K_PASS].bitcast(FP8X4),
+                scales=s_scales[:, first : first + K_PASS],
+                in_=s_grouped[:],
+            )
+
+        def regroup_v(c, h):
+            v_grouped = stage.tile([P, BANK * PACK], BF16, tag="v_grouped", align_bytes=64)
+            src = raw_tiles[("v", c)][:].rearrange("p (t f) -> p t f", t=TILES)
+            nc.vector.tensor_copy(
+                out=v_grouped[:].rearrange("p (b i t) -> p b t i", i=4, t=TILES),
+                in_=src[:, :, h * BANK : (h + 1) * BANK].rearrange("p t (b i) -> p b t i", i=4),
+            )
+            return v_grouped
+
+        def quantise_v(c, h, v_grouped):
+            first = c * E + h * BANK
+            nc.vector.quantize_mx(
+                out=v_codes[:, first : first + BANK].bitcast(FP8X4),
+                scales=v_scales[:, first : first + BANK],
+                in_=v_grouped[:],
+            )
+
+        v_pieces = [(c, h) for c in range(GROUPS) for h in range(HALVES)]
+        first_v_block = len(blocks) - len(v_pieces)
+        prepare(*needs[0])
+        prepare(*needs[1])
+        waiting = None
+        for b, (c, g) in enumerate(blocks):
+            if b + 2 < len(needs):
+                prepare(*needs[b + 2])
+            s_grouped = score_block(c, g)
+            if b >= first_v_block:
+                v_grouped = regroup_v(*v_pieces[b - first_v_block])
+            if waiting is not None:
+                quantise_block(*waiting)
+            if b >= first_v_block:
+                quantise_v(*v_pieces[b - first_v_block], v_grouped)
+            waiting = (c, g, s_grouped)
+        quantise_block(*waiting)
+
+        out_tiles = out.rearrange("(g p t) f -> g t p f", p=P, t=TILES)
+
+        def z_and_exp(g, i):
+            z = [psum.tile([P, BANK], F32, name="bank_z%d" % h, tag="bank") for h in range(HALVES)]
+            for c in range(GROUPS):
+                s_first = (c * GROUPS + g) * K_PASS + i * P
+                for h in range(HALVES):
+                    v_first = c * E + h * BANK
+                    nc.tensor.matmul_mx(
+                        out=z[h][:],
+                        lhsT=s_codes[:, s_first : s_first + P].bitcast(FP8X4),
+                        lhsT_scale=s_scales[:, s_first : s_first + P],
+                        rhs=v_codes[:, v_first : v_first + BANK].bitcast(FP8X4),
+                        rhs_scale=v_scales[:, v_first : v_first + BANK],
+                        start=(c == 0),
+                        stop=(c == GROUPS - 1),
+                    )
+            half_max = small.tile([P, HALVES], F32, tag="half_max")
+            for h in range(HALVES):
+                nc.vector.tensor_reduce(
+                    out=half_max[:, h : h + 1], in_=z[h][:], axis=AXIS.X, op=ALU.max
+                )
+            neg_max = small.tile([P, 1], F32, tag="neg_max")
+            nc.vector.tensor_reduce(
+                out=neg_max[:], in_=half_max[:], axis=AXIS.X, op=ALU.max, negate=True
+            )
+            e_row = rows.tile([P, E], F32, tag="e_row")
+            half_sum = small.tile([P, HALVES], F32, tag="half_sum")
+            for h in range(HALVES):
+                nc.scalar.activation(
+                    out=e_row[:, h * BANK : (h + 1) * BANK],
+                    in_=z[h][:],
+                    func=ACT.Exp,
+                    bias=neg_max[:, 0:1],
+                    scale=1.0,
+                    accum_out=half_sum[:, h : h + 1],
+                )
+            return e_row, half_sum
+
+        def normalise_and_store(g, i, e_row, half_sum):
+            total = small.tile([P, 1], F32, tag="total")
+            nc.vector.tensor_reduce(out=total[:], in_=half_sum[:], axis=AXIS.X, op=ALU.add)
+            inverse = small.tile([P, 1], F32, tag="inverse")
+            nc.vector.reciprocal(out=inverse[:], in_=total[:])
+            nc.gpsimd.tensor_scalar(
+                out=e_row[:],
+                in0=e_row[:],
+                scalar1=inverse[:, 0:1],
+                scalar2=0.0,
+                op0=ALU.mult,
+                op1=ALU.add,
+            )
+            nc.sync.dma_start(out=out_tiles[g, i], in_=e_row[:])
+
+        query_tiles = [(g, i) for g in range(GROUPS) for i in range(TILES)]
+        unfinished = None
+        for g, i in query_tiles:
+            e_row, half_sum = z_and_exp(g, i)
+            if unfinished is not None:
+                normalise_and_store(*unfinished)
+            unfinished = (g, i, e_row, half_sum)
+        normalise_and_store(*unfinished)

@@ -41,6 +41,7 @@ def tile_headattetion_pa_kernel(tc, qm, km, vm, out):
         rows = ctx.enter_context(tc.tile_pool(name="rows", bufs=4))
         small = ctx.enter_context(tc.tile_pool(name="small", bufs=4))
         psum = ctx.enter_context(tc.psum_pool(name="psum", bufs=8))
+        ctx.enter_context(tc.manual_schedule())
 
         k_codes = keep.tile([P, GROUPS * TILES * TILE_WORDS], U32, align_bytes=64)
         k_scales = keep.tile([P, GROUPS * TILES * TILE_WORDS], U8, align_bytes=64)

@@ -25,6 +25,7 @@ TILES = K_PASS // P
 E_PASSES = E // K_PASS
 HALVES = E // BANK
 TILE_WORDS = E // PACK
+LAG = 2
 
 FLOPS = 2 * S * S * E + 2 * S * S * E
 
@@ -38,8 +39,8 @@ def tile_headattetion_pa_kernel(tc, qm, km, vm, out):
         keep = ctx.enter_context(tc.tile_pool(name="keep", bufs=1))
         raw_pool = ctx.enter_context(tc.tile_pool(name="raw", bufs=3 * GROUPS))
         stage = ctx.enter_context(tc.tile_pool(name="stage", bufs=3))
-        rows = ctx.enter_context(tc.tile_pool(name="rows", bufs=4))
-        small = ctx.enter_context(tc.tile_pool(name="small", bufs=4))
+        rows = ctx.enter_context(tc.tile_pool(name="rows", bufs=6))
+        small = ctx.enter_context(tc.tile_pool(name="small", bufs=6))
         psum = ctx.enter_context(tc.psum_pool(name="psum", bufs=8))
         ctx.enter_context(tc.manual_schedule())
 
@@ -59,22 +60,25 @@ def tile_headattetion_pa_kernel(tc, qm, km, vm, out):
                 if operand not in needs:
                     needs.append(operand)
 
-        def load_group(src, group, name):
-            raw = raw_pool.tile([P, TILES * E], BF16, name=name, tag="raw")
-            nc.sync.dma_start(
-                out=raw[:],
-                in_=src[group * K_PASS : (group + 1) * K_PASS, :].rearrange(
-                    "(p t) e -> p (t e)", t=TILES
-                ),
-            )
-            return raw
-
         raw_tiles = {}
         for kind, group in needs:
             src = km if kind == "k" else qm
-            raw_tiles[(kind, group)] = load_group(src, group, "raw_%s%d" % (kind, group))
+            raw = raw_pool.tile([P, TILES * E], BF16, name="raw_%s%d" % (kind, group), tag="raw")
+            tiles = src[group * K_PASS : (group + 1) * K_PASS, :].rearrange(
+                "(p t) e -> t p e", t=TILES
+            )
+            for t in range(TILES):
+                nc.sync.dma_start(out=raw[:, t * E : (t + 1) * E], in_=tiles[t])
+            raw_tiles[(kind, group)] = raw
         for group in range(GROUPS):
-            raw_tiles[("v", group)] = load_group(vm, group, "raw_v%d" % group)
+            raw = raw_pool.tile([P, TILES * E], BF16, name="raw_v%d" % group, tag="raw")
+            nc.sync.dma_start(
+                out=raw[:],
+                in_=vm[group * K_PASS : (group + 1) * K_PASS, :].rearrange(
+                    "(p t) e -> p (t e)", t=TILES
+                ),
+            )
+            raw_tiles[("v", group)] = raw
 
         ident = const.tile([P, P], F32)
         make_identity(nc, ident[:])
@@ -166,7 +170,7 @@ def tile_headattetion_pa_kernel(tc, qm, km, vm, out):
             )
 
         v_pieces = [(c, h) for c in range(GROUPS) for h in range(HALVES)]
-        first_v_block = len(blocks) - len(v_pieces)
+        first_v_block = len(blocks) - len(v_pieces) - 1
         prepare(*needs[0])
         prepare(*needs[1])
         waiting = None
@@ -174,22 +178,23 @@ def tile_headattetion_pa_kernel(tc, qm, km, vm, out):
             if b + 2 < len(needs):
                 prepare(*needs[b + 2])
             s_grouped = score_block(c, g)
-            if b >= first_v_block:
-                v_grouped = regroup_v(*v_pieces[b - first_v_block])
+            piece = b - first_v_block
+            if 0 <= piece < len(v_pieces):
+                v_grouped = regroup_v(*v_pieces[piece])
             if waiting is not None:
                 quantise_block(*waiting)
-            if b >= first_v_block:
-                quantise_v(*v_pieces[b - first_v_block], v_grouped)
+            if 0 <= piece < len(v_pieces):
+                quantise_v(*v_pieces[piece], v_grouped)
             waiting = (c, g, s_grouped)
         quantise_block(*waiting)
 
         out_tiles = out.rearrange("(g p t) f -> g t p f", p=P, t=TILES)
 
-        def z_and_exp(g, i):
+        def z_passes(g, i):
             z = [psum.tile([P, BANK], F32, name="bank_z%d" % h, tag="bank") for h in range(HALVES)]
-            for c in range(GROUPS):
-                s_first = (c * GROUPS + g) * K_PASS + i * P
-                for h in range(HALVES):
+            for h in range(HALVES):
+                for c in range(GROUPS):
+                    s_first = (c * GROUPS + g) * K_PASS + i * P
                     v_first = c * E + h * BANK
                     nc.tensor.matmul_mx(
                         out=z[h][:],
@@ -200,11 +205,17 @@ def tile_headattetion_pa_kernel(tc, qm, km, vm, out):
                         start=(c == 0),
                         stop=(c == GROUPS - 1),
                     )
+            return z
+
+        def maxima_of_halves(z):
             half_max = small.tile([P, HALVES], F32, tag="half_max")
             for h in range(HALVES):
                 nc.vector.tensor_reduce(
                     out=half_max[:, h : h + 1], in_=z[h][:], axis=AXIS.X, op=ALU.max
                 )
+            return half_max
+
+        def exponentials(z, half_max):
             neg_max = small.tile([P, 1], F32, tag="neg_max")
             nc.vector.tensor_reduce(
                 out=neg_max[:], in_=half_max[:], axis=AXIS.X, op=ALU.max, negate=True
@@ -222,26 +233,44 @@ def tile_headattetion_pa_kernel(tc, qm, km, vm, out):
                 )
             return e_row, half_sum
 
-        def normalise_and_store(g, i, e_row, half_sum):
+        def sum_of_halves(half_sum):
             total = small.tile([P, 1], F32, tag="total")
             nc.vector.tensor_reduce(out=total[:], in_=half_sum[:], axis=AXIS.X, op=ALU.add)
+            return total
+
+        def normalise_and_store(g, i, e_row, total, vector_is_free):
             inverse = small.tile([P, 1], F32, tag="inverse")
             nc.vector.reciprocal(out=inverse[:], in_=total[:])
-            nc.gpsimd.tensor_scalar(
-                out=e_row[:],
-                in0=e_row[:],
-                scalar1=inverse[:, 0:1],
-                scalar2=0.0,
-                op0=ALU.mult,
-                op1=ALU.add,
-            )
-            nc.sync.dma_start(out=out_tiles[g, i], in_=e_row[:])
+            if not vector_is_free:
+                nc.gpsimd.tensor_scalar(
+                    out=e_row[:],
+                    in0=e_row[:],
+                    scalar1=inverse[:, 0:1],
+                    scalar2=0.0,
+                    op0=ALU.mult,
+                    op1=ALU.add,
+                )
+                nc.sync.dma_start(out=out_tiles[g, i], in_=e_row[:])
+            else:
+                for h in range(HALVES):
+                    cols = slice(h * BANK, (h + 1) * BANK)
+                    nc.vector.tensor_scalar_mul(
+                        out=e_row[:, cols], in0=e_row[:, cols], scalar1=inverse[:, 0:1]
+                    )
+                    nc.sync.dma_start(out=out_tiles[g, i][:, cols], in_=e_row[:, cols])
 
         query_tiles = [(g, i) for g in range(GROUPS) for i in range(TILES)]
-        unfinished = None
-        for g, i in query_tiles:
-            e_row, half_sum = z_and_exp(g, i)
-            if unfinished is not None:
-                normalise_and_store(*unfinished)
-            unfinished = (g, i, e_row, half_sum)
-        normalise_and_store(*unfinished)
+        issued = []
+        for n in range(len(query_tiles) + LAG):
+            old = issued[n - LAG] if n >= LAG else None
+            if n < len(query_tiles):
+                g, i = query_tiles[n]
+                z = z_passes(g, i)
+                half_max = maxima_of_halves(z)
+            if old is not None:
+                total = sum_of_halves(old[3])
+            if n < len(query_tiles):
+                e_row, half_sum = exponentials(z, half_max)
+                issued.append((g, i, e_row, half_sum))
+            if old is not None:
+                normalise_and_store(old[0], old[1], old[2], total, n >= len(query_tiles))

import math
from contextlib import ExitStack

import concourse.mybir as mybir
from concourse.masks import make_identity

F32 = mybir.dt.float32
BF16 = mybir.dt.bfloat16
U32 = mybir.dt.uint32
U8 = mybir.dt.uint8
FP8X4 = mybir.dt.float8_e4m3fn_x4
ACT = mybir.ActivationFunctionType
ALU = mybir.AluOpType
AXIS = mybir.AxisListType

S = 1536
E = 1024
P = 128
PACK = 4
K_PASS = P * PACK
BANK = 512

GROUPS = S // K_PASS
TILES = K_PASS // P
E_PASSES = E // K_PASS
HALVES = E // BANK
TILE_WORDS = E // PACK
LAG = 2

FLOPS = 2 * S * S * E + 2 * S * S * E


def tile_headattetion_pa_kernel(tc, qm, km, vm, out):
    nc = tc.nc
    inv_sqrt_s = 1.0 / math.sqrt(S)

    with ExitStack() as ctx:
        const = ctx.enter_context(tc.tile_pool(name="const", bufs=1))
        keep = ctx.enter_context(tc.tile_pool(name="keep", bufs=1))
        raw_pool = ctx.enter_context(tc.tile_pool(name="raw", bufs=3 * GROUPS))
        stage = ctx.enter_context(tc.tile_pool(name="stage", bufs=3))
        rows = ctx.enter_context(tc.tile_pool(name="rows", bufs=6))
        small = ctx.enter_context(tc.tile_pool(name="small", bufs=6))
        psum = ctx.enter_context(tc.psum_pool(name="psum", bufs=8))
        ctx.enter_context(tc.manual_schedule())

        k_codes = keep.tile([P, GROUPS * TILES * TILE_WORDS], U32, align_bytes=64)
        k_scales = keep.tile([P, GROUPS * TILES * TILE_WORDS], U8, align_bytes=64)
        q_codes = keep.tile([P, GROUPS * TILES * TILE_WORDS], U32, align_bytes=64)
        q_scales = keep.tile([P, GROUPS * TILES * TILE_WORDS], U8, align_bytes=64)
        v_codes = keep.tile([P, GROUPS * E], U32, align_bytes=64)
        v_scales = keep.tile([P, GROUPS * E], U8, align_bytes=64)
        s_codes = keep.tile([P, GROUPS * S], U32, align_bytes=64)
        s_scales = keep.tile([P, GROUPS * S], U8, align_bytes=64)

        blocks = [(c, g) for g in range(GROUPS) for c in range(GROUPS)]
        needs = []
        for c, g in blocks:
            for operand in (("k", c), ("q", g)):
                if operand not in needs:
                    needs.append(operand)

        raw_tiles = {}
        for kind, group in needs:
            src = km if kind == "k" else qm
            raw = raw_pool.tile([P, TILES * E], BF16, name="raw_%s%d" % (kind, group), tag="raw")
            tiles = src[group * K_PASS : (group + 1) * K_PASS, :].rearrange(
                "(p t) e -> t p e", t=TILES
            )
            for t in range(TILES):
                nc.sync.dma_start(out=raw[:, t * E : (t + 1) * E], in_=tiles[t])
            raw_tiles[(kind, group)] = raw
        for group in range(GROUPS):
            raw = raw_pool.tile([P, TILES * E], BF16, name="raw_v%d" % group, tag="raw")
            nc.sync.dma_start(
                out=raw[:],
                in_=vm[group * K_PASS : (group + 1) * K_PASS, :].rearrange(
                    "(p t) e -> p (t e)", t=TILES
                ),
            )
            raw_tiles[("v", group)] = raw

        ident = const.tile([P, P], F32)
        make_identity(nc, ident[:])

        warm = const.tile([P, 1], F32)
        nc.vector.memset(warm[:], 0.0)
        nc.scalar.activation(out=warm[:], in_=warm[:], func=ACT.Exp)

        def prepare(kind, group):
            raw_words = raw_tiles[(kind, group)][:].bitcast(F32)
            codes, scales = (k_codes, k_scales) if kind == "k" else (q_codes, q_scales)
            grouped = stage.tile([P, TILES * E], BF16, tag="grouped", align_bytes=64)
            grouped_words = grouped[:].bitcast(F32)
            words = E // 2
            for t in range(TILES):
                bank = psum.tile([P, BANK], F32, name="bank_t", tag="bank")
                for j in range(words // P):
                    nc.tensor.transpose(
                        bank[:, j * P : (j + 1) * P],
                        raw_words[:, t * words + j * P : t * words + (j + 1) * P],
                        ident[:],
                    )
                dst = grouped_words[:, t * words : (t + 1) * words].rearrange(
                    "p (a r u) -> p a r u", a=E_PASSES, u=2
                )
                src = bank[:].rearrange("p (a u r) -> p a r u", a=E_PASSES, u=2)
                if t % 2 == 0:
                    nc.scalar.copy(out=dst, in_=src)
                else:
                    nc.vector.tensor_copy(out=dst, in_=src)
            for t in range(TILES):
                first = (group * TILES + t) * TILE_WORDS
                nc.vector.quantize_mx(
                    out=codes[:, first : first + TILE_WORDS].bitcast(FP8X4),
                    scales=scales[:, first : first + TILE_WORDS],
                    in_=grouped[:, t * E : (t + 1) * E],
                )

        def score_block(c, g):
            s_grouped = stage.tile([P, TILES * P * PACK], BF16, tag="s_grouped", align_bytes=64)
            for i in range(TILES):
                bank = psum.tile([P, BANK], F32, name="bank_s", tag="bank")
                for t in range(TILES):
                    for a in range(E_PASSES):
                        k_first = (c * TILES + t) * TILE_WORDS + a * P
                        q_first = (g * TILES + i) * TILE_WORDS + a * P
                        nc.tensor.matmul_mx(
                            out=bank[:, t * P : (t + 1) * P],
                            lhsT=k_codes[:, k_first : k_first + P].bitcast(FP8X4),
                            lhsT_scale=k_scales[:, k_first : k_first + P],
                            rhs=q_codes[:, q_first : q_first + P].bitcast(FP8X4),
                            rhs_scale=q_scales[:, q_first : q_first + P],
                            start=(a == 0),
                            stop=(a == E_PASSES - 1),
                        )
                nc.scalar.activation(
                    out=s_grouped[:, i * BANK : (i + 1) * BANK].rearrange(
                        "p (n t) -> p n t", t=TILES
                    ),
                    in_=bank[:].rearrange("p (t n) -> p n t", t=TILES),
                    func=ACT.Copy,
                    scale=inv_sqrt_s,
                )
            return s_grouped

        def quantise_block(c, g, s_grouped):
            first = (c * GROUPS + g) * K_PASS
            nc.vector.quantize_mx(
                out=s_codes[:, first : first + K_PASS].bitcast(FP8X4),
                scales=s_scales[:, first : first + K_PASS],
                in_=s_grouped[:],
            )

        def regroup_v(c, h):
            v_grouped = stage.tile([P, BANK * PACK], BF16, tag="v_grouped", align_bytes=64)
            src = raw_tiles[("v", c)][:].rearrange("p (t f) -> p t f", t=TILES)
            nc.vector.tensor_copy(
                out=v_grouped[:].rearrange("p (b i t) -> p b t i", i=4, t=TILES),
                in_=src[:, :, h * BANK : (h + 1) * BANK].rearrange("p t (b i) -> p b t i", i=4),
            )
            return v_grouped

        def quantise_v(c, h, v_grouped):
            first = c * E + h * BANK
            nc.vector.quantize_mx(
                out=v_codes[:, first : first + BANK].bitcast(FP8X4),
                scales=v_scales[:, first : first + BANK],
                in_=v_grouped[:],
            )

        v_pieces = [(c, h) for c in range(GROUPS) for h in range(HALVES)]
        first_v_block = len(blocks) - len(v_pieces) - 1
        prepare(*needs[0])
        prepare(*needs[1])
        waiting = None
        for b, (c, g) in enumerate(blocks):
            if b + 2 < len(needs):
                prepare(*needs[b + 2])
            s_grouped = score_block(c, g)
            piece = b - first_v_block
            if 0 <= piece < len(v_pieces):
                v_grouped = regroup_v(*v_pieces[piece])
            if waiting is not None:
                quantise_block(*waiting)
            if 0 <= piece < len(v_pieces):
                quantise_v(*v_pieces[piece], v_grouped)
            waiting = (c, g, s_grouped)
        quantise_block(*waiting)

        out_tiles = out.rearrange("(g p t) f -> g t p f", p=P, t=TILES)

        def z_passes(g, i):
            z = [psum.tile([P, BANK], F32, name="bank_z%d" % h, tag="bank") for h in range(HALVES)]
            for h in range(HALVES):
                for c in range(GROUPS):
                    s_first = (c * GROUPS + g) * K_PASS + i * P
                    v_first = c * E + h * BANK
                    nc.tensor.matmul_mx(
                        out=z[h][:],
                        lhsT=s_codes[:, s_first : s_first + P].bitcast(FP8X4),
                        lhsT_scale=s_scales[:, s_first : s_first + P],
                        rhs=v_codes[:, v_first : v_first + BANK].bitcast(FP8X4),
                        rhs_scale=v_scales[:, v_first : v_first + BANK],
                        start=(c == 0),
                        stop=(c == GROUPS - 1),
                    )
            return z

        def maxima_of_halves(z):
            half_max = small.tile([P, HALVES], F32, tag="half_max")
            for h in range(HALVES):
                nc.vector.tensor_reduce(
                    out=half_max[:, h : h + 1], in_=z[h][:], axis=AXIS.X, op=ALU.max
                )
            return half_max

        def exponentials(z, half_max):
            neg_max = small.tile([P, 1], F32, tag="neg_max")
            nc.vector.tensor_reduce(
                out=neg_max[:], in_=half_max[:], axis=AXIS.X, op=ALU.max, negate=True
            )
            e_row = rows.tile([P, E], F32, tag="e_row")
            half_sum = small.tile([P, HALVES], F32, tag="half_sum")
            for h in range(HALVES):
                nc.scalar.activation(
                    out=e_row[:, h * BANK : (h + 1) * BANK],
                    in_=z[h][:],
                    func=ACT.Exp,
                    bias=neg_max[:, 0:1],
                    scale=1.0,
                    accum_out=half_sum[:, h : h + 1],
                )
            return e_row, half_sum

        def sum_of_halves(half_sum):
            total = small.tile([P, 1], F32, tag="total")
            nc.vector.tensor_reduce(out=total[:], in_=half_sum[:], axis=AXIS.X, op=ALU.add)
            return total

        def normalise_and_store(g, i, e_row, total, vector_is_free):
            inverse = small.tile([P, 1], F32, tag="inverse")
            nc.vector.reciprocal(out=inverse[:], in_=total[:])
            if not vector_is_free:
                nc.gpsimd.tensor_scalar(
                    out=e_row[:],
                    in0=e_row[:],
                    scalar1=inverse[:, 0:1],
                    scalar2=0.0,
                    op0=ALU.mult,
                    op1=ALU.add,
                )
                nc.sync.dma_start(out=out_tiles[g, i], in_=e_row[:])
            else:
                for h in range(HALVES):
                    cols = slice(h * BANK, (h + 1) * BANK)
                    nc.vector.tensor_scalar_mul(
                        out=e_row[:, cols], in0=e_row[:, cols], scalar1=inverse[:, 0:1]
                    )
                    nc.sync.dma_start(out=out_tiles[g, i][:, cols], in_=e_row[:, cols])

        query_tiles = [(g, i) for g in range(GROUPS) for i in range(TILES)]
        issued = []
        for n in range(len(query_tiles) + LAG):
            old = issued[n - LAG] if n >= LAG else None
            if n < len(query_tiles):
                g, i = query_tiles[n]
                z = z_passes(g, i)
                half_max = maxima_of_halves(z)
            if old is not None:
                total = sum_of_halves(old[3])
            if n < len(query_tiles):
                e_row, half_sum = exponentials(z, half_max)
                issued.append((g, i, e_row, half_sum))
            if old is not None:
                normalise_and_store(old[0], old[1], old[2], total, n >= len(query_tiles))
